import numpy as np
import ml_dtypes


def mxq(x, axis, fmt="e4m3"):
    dtype, down = {"e4m3": (ml_dtypes.float8_e4m3fn, 7), "e5m2": (ml_dtypes.float8_e5m2, 14)}[fmt]
    v = np.moveaxis(np.asarray(x, np.float32).astype(ml_dtypes.bfloat16).astype(np.float64), axis, -1)
    blocks = v.reshape(v.shape[:-1] + (-1, 32))
    amax = np.abs(blocks).max(-1, keepdims=True)
    byte = np.maximum(np.where(amax > 0, np.frexp(amax)[1] - 1 + 127, 0) - down, 1)
    scale = np.exp2(byte - 127.0)
    codes = (blocks / scale).astype(np.float32).astype(dtype).astype(np.float64)
    return np.moveaxis((codes * scale).reshape(v.shape), -1, axis)


WIDE = False


def mx_kscale(k):
    if not WIDE:
        return np.ones(k)
    levels = np.array([10, -10, 5, -5, 0])
    a = np.random.permutation(np.resize(levels, k // 512 * 4)).reshape(k // 512, 4)
    idx = np.arange(k)
    return np.exp2(a[idx // 512, idx % 128 // 32])


BF16 = ml_dtypes.bfloat16


def bf(x):
    return np.asarray(x, np.float32).astype(BF16)


def f64(x):
    return np.asarray(x).astype(np.float64)


E2M1 = np.array([0.0, 0.5, 1.0, 1.5, 2.0, 3.0, 4.0, 6.0, -0.0, -0.5, -1.0, -1.5, -2.0, -3.0, -4.0, -6.0])


def pack_weight(w, fmt):
    k, n = w.shape
    w = f64(bf(w)).reshape(k // 32, 32, n)
    amax = np.abs(w).max(1)
    if fmt == "e4m3":
        byte = np.frexp(amax)[1] - 1 + 127 - 7
    else:
        mant, ex = np.frexp(amax / 6.0)
        byte = np.where(mant > 0.5, ex, ex - 1) + 127
    byte = np.clip(np.where(amax > 0, byte, 1), 1, 254)
    scaled = (w * np.exp2(127.0 - byte)[:, None, :]).reshape(k, n).astype(np.float32)
    by_word = np.ascontiguousarray(scaled.reshape(k // 512, 128, 4, n).transpose(0, 1, 3, 2))
    if fmt == "e4m3":
        words = by_word.astype(ml_dtypes.float8_e4m3fn).view(np.uint8)
    else:
        c = by_word.astype(ml_dtypes.float4_e2m1fn).view(np.uint8) & 0xF
        words = c[..., 0::2] | (c[..., 1::2] << 4)
    return np.ascontiguousarray(words), np.ascontiguousarray(byte.astype(np.uint8).reshape(k // 512, 16, n))


def unpack_weight(words, scales, fmt):
    g, p, n, _ = words.shape
    if fmt == "e4m3":
        vals = np.ascontiguousarray(words).view(ml_dtypes.float8_e4m3fn).astype(np.float64)
    else:
        nib = np.empty((g, p, n, 4), np.uint8)
        nib[..., 0::2] = words & 0xF
        nib[..., 1::2] = words >> 4
        vals = E2M1[nib]
    vals = vals * np.repeat(np.exp2(scales.astype(np.float64) - 127.0), 8, axis=1)[..., None]
    return vals.transpose(0, 1, 3, 2).reshape(g * 512, n)


B, S, H, I, G = 4, 1024, 512, 1024, 4
T = B * S
FMT = "e4m3"


def grouped_linear(xf, words, scales, b, din, dout):
    w = unpack_weight(words, scales, FMT).reshape(G, din, dout)
    xg = xf.reshape(G, -1, din)
    y = (mxq(xg, 2, "e4m3") @ w) + b[:, None, :]
    return y.reshape(-1, dout)


def setup_inputs():
    s, t = mx_kscale(H), mx_kscale(I)
    hf = bf(np.random.standard_normal((T, H)) * s)
    g1 = np.random.standard_normal((G, I, H)) / np.sqrt(H) / s[None, None, :] * t[None, :, None]
    g1_b = bf(np.random.standard_normal((G, I)) * 0.3 * t[None, :])
    g2 = np.random.standard_normal((G, H, I)) / np.sqrt(I) / t[None, None, :]
    g2_b = bf(np.random.standard_normal((G, H)) * 0.3)
    g1_words, g1_scales = pack_weight(np.ascontiguousarray(g1.swapaxes(1, 2)).reshape(-1, I), FMT)
    g2_words, g2_scales = pack_weight(np.ascontiguousarray(g2.swapaxes(1, 2)).reshape(-1, H), FMT)
    return {"hf": hf,
            "g1_w_words": g1_words,
            "g1_w_scales": g1_scales,
            "g1_b": g1_b,
            "g2_w_words": g2_words,
            "g2_w_scales": g2_scales,
            "g2_b": g2_b}


def reference(hf, g1_w_words, g1_w_scales, g1_b, g2_w_words, g2_w_scales, g2_b):
    y = grouped_linear(f64(hf), g1_w_words, g1_w_scales, f64(g1_b), H, I)
    return grouped_linear(y, g2_w_words, g2_w_scales, f64(g2_b), I, H)

@@ -1,0 +1,219 @@
+from contextlib import ExitStack
+
+import concourse.mybir as mybir
+from concourse.masks import make_identity
+
+F32 = mybir.dt.float32
+BF16 = mybir.dt.bfloat16
+I32 = mybir.dt.int32
+U32 = mybir.dt.uint32
+U8 = mybir.dt.uint8
+FP8X4 = mybir.dt.float8_e4m3fn_x4
+ADD = mybir.AluOpType.add
+MULT = mybir.AluOpType.mult
+
+P = 128
+PACK = 4
+K_PASS = P * PACK
+GROUPS = 4
+HID = 512
+MID = 1024
+MID_PASSES = MID // K_PASS
+TILES = 1024 // P
+PAIR = 2
+STEPS = GROUPS * TILES // PAIR
+STEPS_PER_GROUP = TILES // PAIR
+X_LEAD = 2
+
+FLOPS = 2 * GROUPS * 1024 * (HID * MID + MID * HID)
+
+
+def tile_dummytemodel_pa_t_e_kernel(
+    tc, hf, g1_w_words, g1_w_scales, g1_b, g2_w_words, g2_w_scales, g2_b, out
+):
+    nc = tc.nc
+    hf_tiles = hf.rearrange("(e p i) k -> e p i k", e=GROUPS, i=TILES)
+    out_tiles = out.rearrange("(e p i) n -> e p i n", e=GROUPS, i=TILES)
+
+    with ExitStack() as ctx:
+        keep = ctx.enter_context(tc.tile_pool(name="keep", bufs=1))
+        work = ctx.enter_context(tc.tile_pool(name="work", bufs=2))
+        psum_y = ctx.enter_context(tc.psum_pool(name="psum_y", bufs=PAIR * MID_PASSES))
+        psum_yt = ctx.enter_context(tc.psum_pool(name="psum_yt", bufs=PAIR))
+        psum_xo = ctx.enter_context(tc.psum_pool(name="psum_xo", bufs=2))
+        ctx.enter_context(tc.manual_schedule())
+
+        x_sb = keep.tile([P, GROUPS, TILES, HID], BF16)
+        w1 = keep.tile([P, GROUPS, MID], U32, align_bytes=64)
+        w2 = keep.tile([P, GROUPS, MID_PASSES, HID], U32, align_bytes=64)
+        w1_scales = keep.tile([P, MID], U8, align_bytes=64)
+        w2_scales = keep.tile([P, MID_PASSES, HID], U8, align_bytes=64)
+        b1_rows = keep.tile([P, GROUPS, MID], BF16)
+        b1_sorted = keep.tile([P, GROUPS, MID_PASSES, PACK, P], BF16)
+        b2_rows = keep.tile([P, GROUPS, HID], BF16)
+        x_codes = keep.tile([P, STEPS, PAIR, P], U32, align_bytes=64)
+        x_scales = keep.tile([P, STEPS, PAIR, P], U8, align_bytes=64)
+        ident_f32 = keep.tile([P, P], F32)
+        ident_bf16 = keep.tile([P, P], BF16)
+
+        nc.vector.memset(w1_scales[:].bitcast(I32), 0)
+        nc.vector.memset(w2_scales[:].bitcast(I32), 0)
+        make_identity(nc, ident_f32[:])
+        make_identity(nc, ident_bf16[:])
+
+        def load_tokens(e, first, count):
+            nc.sync.dma_start(out=x_sb[:, e, first : first + count, :], in_=hf_tiles[e][:, first : first + count, :])
+
+        def load_w1(e):
+            nc.sync.dma_start(
+                out=w1[:, e, :].bitcast(I32), in_=g1_w_words[e].rearrange("p n t -> p (n t)").bitcast(I32)
+            )
+
+        def load_w2(e):
+            nc.sync.dma_start(
+                out=w2[:, e, :, :].bitcast(I32),
+                in_=g2_w_words[MID_PASSES * e : MID_PASSES * (e + 1)].rearrange("c p n t -> p c (n t)").bitcast(I32),
+            )
+
+        def load_b1(e):
+            nc.sync.dma_start(out=b1_rows[:, e, :], in_=g1_b[e].partition_broadcast(P))
+
+        load_tokens(0, 0, PAIR)
+        load_tokens(0, PAIR, PAIR)
+        for quadrant in range(4):
+            rows = slice(4 * quadrant, 4 * quadrant + 4)
+            nc.sync.dma_start(
+                out=w1_scales[32 * quadrant : 32 * quadrant + 16, :].bitcast(I32),
+                in_=g1_w_scales[:, rows, :].bitcast(I32),
+            )
+        load_w1(0)
+        load_b1(0)
+        load_tokens(0, 2 * PAIR, TILES - 2 * PAIR)
+        for c in range(MID_PASSES):
+            for quadrant in range(4):
+                rows = slice(4 * quadrant, 4 * quadrant + 4)
+                nc.sync.dma_start(
+                    out=w2_scales[32 * quadrant : 32 * quadrant + 16, c, :].bitcast(I32),
+                    in_=g2_w_scales[c : GROUPS * MID_PASSES : MID_PASSES, rows, :].bitcast(I32),
+                )
+        load_w2(0)
+        nc.sync.dma_start(
+            out=b2_rows[:].rearrange("q e n -> q (e n)"), in_=g2_b.rearrange("e n -> (e n)").partition_broadcast(P)
+        )
+        for e in range(1, GROUPS):
+            load_b1(e)
+            load_tokens(e, 0, TILES)
+            load_w1(e)
+            load_w2(e)
+
+        x_grouped = {}
+        y_sorted = {}
+        y_grouped = {}
+        y_codes = {}
+        y_scales = {}
+
+        def sort_b1(e):
+            nc.gpsimd.tensor_scalar(
+                out=b1_sorted[:, e],
+                in0=b1_rows[:, e, :].rearrange("q (c p t) -> q c t p", c=MID_PASSES, t=PACK),
+                scalar1=1.0,
+                scalar2=0.0,
+                op0=MULT,
+                op1=ADD,
+            )
+
+        def transpose_x(s):
+            e, first = s // STEPS_PER_GROUP, PAIR * (s % STEPS_PER_GROUP)
+            x_t = psum_xo.tile([P, PAIR, 2, P], F32, tag="xo")
+            for j in range(PAIR):
+                words = x_sb[:, e, first + j, :].bitcast(F32)
+                for u in range(2):
+                    nc.tensor.transpose(out=x_t[:, j, u, :], in_=words[:, u : HID // 2 : 2], identity=ident_f32[:])
+            x_grouped[s] = work.tile([P, PAIR * P * PACK], BF16, align_bytes=64, name="x_grouped")
+            nc.scalar.copy(
+                out=x_grouped[s][:].bitcast(F32).rearrange("p (j r u) -> p j r u", j=PAIR, u=2),
+                in_=x_t[:].rearrange("p j u r -> p j r u"),
+            )
+
+        def quantise_x(s):
+            nc.vector.quantize_mx(
+                out=x_codes[:, s].rearrange("p j r -> p (j r)").bitcast(FP8X4),
+                scales=x_scales[:, s].rearrange("p j r -> p (j r)"),
+                in_=x_grouped[s][:],
+            )
+
+        def layer1(s):
+            e = s // STEPS_PER_GROUP
+            for j in range(PAIR):
+                for c in range(MID_PASSES):
+                    columns = slice(K_PASS * c, K_PASS * (c + 1))
+                    y_ps = psum_y.tile([P, K_PASS], F32)
+                    nc.tensor.matmul_mx(
+                        out=y_ps[:],
+                        lhsT=x_codes[:, s, j, :].bitcast(FP8X4),
+                        lhsT_scale=x_scales[:, s, j, :],
+                        rhs=w1[:, e, columns].bitcast(FP8X4),
+                        rhs_scale=w1_scales[4 * e : P, columns],
+                        start=True,
+                        stop=True,
+                    )
+                    y_sorted[s, j, c] = work.tile([P, PACK, P], BF16, name="y_sorted", bufs=2 * PAIR * MID_PASSES)
+                    nc.vector.tensor_tensor(
+                        out=y_sorted[s, j, c][:],
+                        in0=y_ps[:].rearrange("q (p t) -> q t p", t=PACK),
+                        in1=b1_sorted[:, e, c],
+                        op=ADD,
+                    )
+
+        def transpose_y(s):
+            y_grouped[s] = work.tile([P, PAIR, MID_PASSES, P, PACK], BF16, align_bytes=64, name="y_grouped")
+            for j in range(PAIR):
+                y_t = psum_yt.tile([P, MID_PASSES, PACK, P], BF16)
+                for c in range(MID_PASSES):
+                    for t in range(PACK):
+                        nc.tensor.transpose(out=y_t[:, c, t, :], in_=y_sorted[s, j, c][:, t, :], identity=ident_bf16[:])
+                nc.scalar.copy(out=y_grouped[s][:, j], in_=y_t[:].rearrange("p c t r -> p c r t"))
+
+        def quantise_y(s):
+            y_codes[s] = work.tile([P, PAIR, MID_PASSES, P], U32, align_bytes=64, name="y_codes")
+            y_scales[s] = work.tile([P, PAIR, MID_PASSES, P], U8, align_bytes=64, name="y_scales")
+            nc.vector.quantize_mx(
+                out=y_codes[s][:].rearrange("p j c r -> p (j c r)").bitcast(FP8X4),
+                scales=y_scales[s][:].rearrange("p j c r -> p (j c r)"),
+                in_=y_grouped[s][:].rearrange("p j c r t -> p (j c r t)"),
+            )
+
+        def layer2(s):
+            e, first = s // STEPS_PER_GROUP, PAIR * (s % STEPS_PER_GROUP)
+            o_sb = work.tile([P, PAIR, HID], F32, bufs=3)
+            for j in range(PAIR):
+                o_ps = psum_xo.tile([P, HID], F32, tag="xo")
+                for c in range(MID_PASSES):
+                    nc.tensor.matmul_mx(
+                        out=o_ps[:],
+                        lhsT=y_codes[s][:, j, c, :].bitcast(FP8X4),
+                        lhsT_scale=y_scales[s][:, j, c, :],
+                        rhs=w2[:, e, c, :].bitcast(FP8X4),
+                        rhs_scale=w2_scales[4 * e : P, c, :],
+                        start=(c == 0),
+                        stop=(c == MID_PASSES - 1),
+                    )
+                nc.scalar.copy(out=o_sb[:, j, :], in_=o_ps[:])
+                nc.gpsimd.tensor_tensor(out=o_sb[:, j, :], in0=o_sb[:, j, :], in1=b2_rows[:, e, :], op=ADD)
+            nc.sync.dma_start(out=out_tiles[e][:, first : first + PAIR, :], in_=o_sb[:])
+
+        for s in range(-X_LEAD, STEPS + 1):
+            if 0 <= s < STEPS:
+                transpose_y(s)
+            if s + X_LEAD < STEPS:
+                if (s + X_LEAD) % STEPS_PER_GROUP == 0:
+                    sort_b1((s + X_LEAD) // STEPS_PER_GROUP)
+                transpose_x(s + X_LEAD)
+            if 0 <= s + 1 < STEPS:
+                layer1(s + 1)
+            if s + X_LEAD < STEPS:
+                quantise_x(s + X_LEAD)
+            if 0 <= s < STEPS:
+                quantise_y(s)
+            if 0 <= s - 1:
+                layer2(s - 1)

@@ -23,7 +23,11 @@ TILES = 1024 // P
 PAIR = 2
 STEPS = GROUPS * TILES // PAIR
 STEPS_PER_GROUP = TILES // PAIR
-X_LEAD = 2
+X_TO_LAYER1 = 2
+LAYER1_TO_Y = 2
+Y_TO_LAYER2 = 1
+
+Y_SORTED_BUFS = (LAYER1_TO_Y + 1) * PAIR * MID_PASSES
 
 FLOPS = 2 * GROUPS * 1024 * (HID * MID + MID * HID)
 
@@ -38,9 +42,9 @@ def tile_dummytemodel_pa_t_e_kernel(
     with ExitStack() as ctx:
         keep = ctx.enter_context(tc.tile_pool(name="keep", bufs=1))
         work = ctx.enter_context(tc.tile_pool(name="work", bufs=2))
-        psum_y = ctx.enter_context(tc.psum_pool(name="psum_y", bufs=PAIR * MID_PASSES))
+        psum_xy = ctx.enter_context(tc.psum_pool(name="psum_xy", bufs=4))
         psum_yt = ctx.enter_context(tc.psum_pool(name="psum_yt", bufs=PAIR))
-        psum_xo = ctx.enter_context(tc.psum_pool(name="psum_xo", bufs=2))
+        psum_o = ctx.enter_context(tc.psum_pool(name="psum_o", bufs=PAIR))
         ctx.enter_context(tc.manual_schedule())
 
         x_sb = keep.tile([P, GROUPS, TILES, HID], BF16)
@@ -78,8 +82,8 @@ def tile_dummytemodel_pa_t_e_kernel(
         def load_b1(e):
             nc.sync.dma_start(out=b1_rows[:, e, :], in_=g1_b[e].partition_broadcast(P))
 
-        load_tokens(0, 0, PAIR)
-        load_tokens(0, PAIR, PAIR)
+        for first in range(0, TILES, PAIR):
+            load_tokens(0, first, PAIR)
         for quadrant in range(4):
             rows = slice(4 * quadrant, 4 * quadrant + 4)
             nc.sync.dma_start(
@@ -88,7 +92,7 @@ def tile_dummytemodel_pa_t_e_kernel(
             )
         load_w1(0)
         load_b1(0)
-        load_tokens(0, 2 * PAIR, TILES - 2 * PAIR)
+        load_tokens(1, 0, TILES)
         for c in range(MID_PASSES):
             for quadrant in range(4):
                 rows = slice(4 * quadrant, 4 * quadrant + 4)
@@ -102,8 +106,9 @@ def tile_dummytemodel_pa_t_e_kernel(
         )
         for e in range(1, GROUPS):
             load_b1(e)
-            load_tokens(e, 0, TILES)
             load_w1(e)
+            if e + 1 < GROUPS:
+                load_tokens(e + 1, 0, TILES)
             load_w2(e)
 
         x_grouped = {}
@@ -124,7 +129,7 @@ def tile_dummytemodel_pa_t_e_kernel(
 
         def transpose_x(s):
             e, first = s // STEPS_PER_GROUP, PAIR * (s % STEPS_PER_GROUP)
-            x_t = psum_xo.tile([P, PAIR, 2, P], F32, tag="xo")
+            x_t = psum_xy.tile([P, PAIR, 2, P], F32, tag="xy")
             for j in range(PAIR):
                 words = x_sb[:, e, first + j, :].bitcast(F32)
                 for u in range(2):
@@ -147,7 +152,7 @@ def tile_dummytemodel_pa_t_e_kernel(
             for j in range(PAIR):
                 for c in range(MID_PASSES):
                     columns = slice(K_PASS * c, K_PASS * (c + 1))
-                    y_ps = psum_y.tile([P, K_PASS], F32)
+                    y_ps = psum_xy.tile([P, K_PASS], F32, tag="xy")
                     nc.tensor.matmul_mx(
                         out=y_ps[:],
                         lhsT=x_codes[:, s, j, :].bitcast(FP8X4),
@@ -157,7 +162,7 @@ def tile_dummytemodel_pa_t_e_kernel(
                         start=True,
                         stop=True,
                     )
-                    y_sorted[s, j, c] = work.tile([P, PACK, P], BF16, name="y_sorted", bufs=2 * PAIR * MID_PASSES)
+                    y_sorted[s, j, c] = work.tile([P, PACK, P], BF16, name="y_sorted", bufs=Y_SORTED_BUFS)
                     nc.vector.tensor_tensor(
                         out=y_sorted[s, j, c][:],
                         in0=y_ps[:].rearrange("q (p t) -> q t p", t=PACK),
@@ -187,7 +192,7 @@ def tile_dummytemodel_pa_t_e_kernel(
             e, first = s // STEPS_PER_GROUP, PAIR * (s % STEPS_PER_GROUP)
             o_sb = work.tile([P, PAIR, HID], F32, bufs=3)
             for j in range(PAIR):
-                o_ps = psum_xo.tile([P, HID], F32, tag="xo")
+                o_ps = psum_o.tile([P, HID], F32)
                 for c in range(MID_PASSES):
                     nc.tensor.matmul_mx(
                         out=o_ps[:],
@@ -202,18 +207,21 @@ def tile_dummytemodel_pa_t_e_kernel(
                 nc.gpsimd.tensor_tensor(out=o_sb[:, j, :], in0=o_sb[:, j, :], in1=b2_rows[:, e, :], op=ADD)
             nc.sync.dma_start(out=out_tiles[e][:, first : first + PAIR, :], in_=o_sb[:])
 
-        for s in range(-X_LEAD, STEPS + 1):
-            if 0 <= s < STEPS:
-                transpose_y(s)
-            if s + X_LEAD < STEPS:
-                if (s + X_LEAD) % STEPS_PER_GROUP == 0:
-                    sort_b1((s + X_LEAD) // STEPS_PER_GROUP)
-                transpose_x(s + X_LEAD)
-            if 0 <= s + 1 < STEPS:
-                layer1(s + 1)
-            if s + X_LEAD < STEPS:
-                quantise_x(s + X_LEAD)
-            if 0 <= s < STEPS:
-                quantise_y(s)
-            if 0 <= s - 1:
-                layer2(s - 1)
+        for r in range(-LAYER1_TO_Y - X_TO_LAYER1, STEPS + Y_TO_LAYER2):
+            x_step = r + LAYER1_TO_Y + X_TO_LAYER1
+            layer1_step = r + LAYER1_TO_Y
+            layer2_step = r - Y_TO_LAYER2
+            if x_step < STEPS:
+                if x_step % STEPS_PER_GROUP == 0:
+                    sort_b1(x_step // STEPS_PER_GROUP)
+                transpose_x(x_step)
+            if 0 <= r < STEPS:
+                transpose_y(r)
+            if 0 <= layer1_step < STEPS:
+                layer1(layer1_step)
+            if x_step < STEPS:
+                quantise_x(x_step)
+            if 0 <= r < STEPS:
+                quantise_y(r)
+            if 0 <= layer2_step:
+                layer2(layer2_step)

@@ -203,8 +203,7 @@ def tile_dummytemodel_pa_t_e_kernel(
                         start=(c == 0),
                         stop=(c == MID_PASSES - 1),
                     )
-                nc.scalar.copy(out=o_sb[:, j, :], in_=o_ps[:])
-                nc.gpsimd.tensor_tensor(out=o_sb[:, j, :], in0=o_sb[:, j, :], in1=b2_rows[:, e, :], op=ADD)
+                nc.vector.tensor_tensor(out=o_sb[:, j, :], in0=o_ps[:], in1=b2_rows[:, e, :], op=ADD)
             nc.sync.dma_start(out=out_tiles[e][:, first : first + PAIR, :], in_=o_sb[:])
 
         for r in range(-LAYER1_TO_Y - X_TO_LAYER1, STEPS + Y_TO_LAYER2):

@@ -10,7 +10,7 @@ U32 = mybir.dt.uint32
 U8 = mybir.dt.uint8
 FP8X4 = mybir.dt.float8_e4m3fn_x4
 ADD = mybir.AluOpType.add
-MULT = mybir.AluOpType.mult
+IDENTITY = mybir.ActivationFunctionType.Identity
 
 P = 128
 PACK = 4
@@ -20,14 +20,10 @@ HID = 512
 MID = 1024
 MID_PASSES = MID // K_PASS
 TILES = 1024 // P
-PAIR = 2
-STEPS = GROUPS * TILES // PAIR
-STEPS_PER_GROUP = TILES // PAIR
-X_TO_LAYER1 = 2
-LAYER1_TO_Y = 2
-Y_TO_LAYER2 = 1
-
-Y_SORTED_BUFS = (LAYER1_TO_Y + 1) * PAIR * MID_PASSES
+QUAD = 4
+TOK = QUAD * P
+STEPS = GROUPS * TILES // QUAD
+STEPS_PER_GROUP = TILES // QUAD
 
 FLOPS = 2 * GROUPS * 1024 * (HID * MID + MID * HID)
 
@@ -42,35 +38,33 @@ def tile_dummytemodel_pa_t_e_kernel(
     with ExitStack() as ctx:
         keep = ctx.enter_context(tc.tile_pool(name="keep", bufs=1))
         work = ctx.enter_context(tc.tile_pool(name="work", bufs=2))
-        psum_xy = ctx.enter_context(tc.psum_pool(name="psum_xy", bufs=4))
-        psum_yt = ctx.enter_context(tc.psum_pool(name="psum_yt", bufs=PAIR))
-        psum_o = ctx.enter_context(tc.psum_pool(name="psum_o", bufs=PAIR))
+        psum_x = ctx.enter_context(tc.psum_pool(name="psum_x", bufs=2))
+        psum_y = ctx.enter_context(tc.psum_pool(name="psum_y", bufs=4))
+        psum_o = ctx.enter_context(tc.psum_pool(name="psum_o", bufs=2))
         ctx.enter_context(tc.manual_schedule())
 
         x_sb = keep.tile([P, GROUPS, TILES, HID], BF16)
-        w1 = keep.tile([P, GROUPS, MID], U32, align_bytes=64)
+        w1_raw = keep.tile([P, GROUPS, MID], U32, align_bytes=64)
+        w1 = keep.tile([P, GROUPS, MID_PASSES, PACK, P], U32, align_bytes=64)
         w2 = keep.tile([P, GROUPS, MID_PASSES, HID], U32, align_bytes=64)
-        w1_scales = keep.tile([P, MID], U8, align_bytes=64)
+        w1_scales_raw = keep.tile([P, MID], U8, align_bytes=64)
+        w1_scales = keep.tile([P, MID_PASSES, PACK, P], U8, align_bytes=64)
         w2_scales = keep.tile([P, MID_PASSES, HID], U8, align_bytes=64)
-        b1_rows = keep.tile([P, GROUPS, MID], BF16)
-        b1_sorted = keep.tile([P, GROUPS, MID_PASSES, PACK, P], BF16)
+        b1_raw = keep.tile([P, GROUPS * MID_PASSES, PACK], BF16)
+        b1 = keep.tile([P, GROUPS * MID_PASSES, PACK], F32)
         b2_rows = keep.tile([P, GROUPS, HID], BF16)
-        x_codes = keep.tile([P, STEPS, PAIR, P], U32, align_bytes=64)
-        x_scales = keep.tile([P, STEPS, PAIR, P], U8, align_bytes=64)
         ident_f32 = keep.tile([P, P], F32)
-        ident_bf16 = keep.tile([P, P], BF16)
 
-        nc.vector.memset(w1_scales[:].bitcast(I32), 0)
+        nc.vector.memset(w1_scales_raw[:].bitcast(I32), 0)
         nc.vector.memset(w2_scales[:].bitcast(I32), 0)
         make_identity(nc, ident_f32[:])
-        make_identity(nc, ident_bf16[:])
 
         def load_tokens(e, first, count):
             nc.sync.dma_start(out=x_sb[:, e, first : first + count, :], in_=hf_tiles[e][:, first : first + count, :])
 
         def load_w1(e):
             nc.sync.dma_start(
-                out=w1[:, e, :].bitcast(I32), in_=g1_w_words[e].rearrange("p n t -> p (n t)").bitcast(I32)
+                out=w1_raw[:, e, :].bitcast(I32), in_=g1_w_words[e].rearrange("p n t -> p (n t)").bitcast(I32)
             )
 
         def load_w2(e):
@@ -79,20 +73,17 @@ def tile_dummytemodel_pa_t_e_kernel(
                 in_=g2_w_words[MID_PASSES * e : MID_PASSES * (e + 1)].rearrange("c p n t -> p c (n t)").bitcast(I32),
             )
 
-        def load_b1(e):
-            nc.sync.dma_start(out=b1_rows[:, e, :], in_=g1_b[e].partition_broadcast(P))
-
-        for first in range(0, TILES, PAIR):
-            load_tokens(0, first, PAIR)
+        for first in range(0, QUAD, 2):
+            load_tokens(0, first, 2)
         for quadrant in range(4):
             rows = slice(4 * quadrant, 4 * quadrant + 4)
             nc.sync.dma_start(
-                out=w1_scales[32 * quadrant : 32 * quadrant + 16, :].bitcast(I32),
+                out=w1_scales_raw[32 * quadrant : 32 * quadrant + 16, :].bitcast(I32),
                 in_=g1_w_scales[:, rows, :].bitcast(I32),
             )
         load_w1(0)
-        load_b1(0)
-        load_tokens(1, 0, TILES)
+        nc.sync.dma_start(out=b1_raw[:], in_=g1_b.rearrange("e (c p t) -> p (e c) t", c=MID_PASSES, t=PACK))
+        load_tokens(0, QUAD, QUAD)
         for c in range(MID_PASSES):
             for quadrant in range(4):
                 rows = slice(4 * quadrant, 4 * quadrant + 4)
@@ -101,126 +92,140 @@ def tile_dummytemodel_pa_t_e_kernel(
                     in_=g2_w_scales[c : GROUPS * MID_PASSES : MID_PASSES, rows, :].bitcast(I32),
                 )
         load_w2(0)
+        load_w1(1)
         nc.sync.dma_start(
             out=b2_rows[:].rearrange("q e n -> q (e n)"), in_=g2_b.rearrange("e n -> (e n)").partition_broadcast(P)
         )
-        for e in range(1, GROUPS):
-            load_b1(e)
+        load_tokens(1, 0, TILES)
+        load_w2(1)
+        for e in range(2, GROUPS):
             load_w1(e)
-            if e + 1 < GROUPS:
-                load_tokens(e + 1, 0, TILES)
+            load_tokens(e, 0, TILES)
             load_w2(e)
 
         x_grouped = {}
-        y_sorted = {}
+        x_codes = {}
+        x_scales = {}
+        y_plain = {}
         y_grouped = {}
         y_codes = {}
         y_scales = {}
+        o_sb = {}
+        o_ps = {}
 
-        def sort_b1(e):
-            nc.gpsimd.tensor_scalar(
-                out=b1_sorted[:, e],
-                in0=b1_rows[:, e, :].rearrange("q (c p t) -> q c t p", c=MID_PASSES, t=PACK),
-                scalar1=1.0,
-                scalar2=0.0,
-                op0=MULT,
-                op1=ADD,
+        def sort_w1_scales():
+            nc.vector.tensor_copy(
+                out=w1_scales[:], in_=w1_scales_raw[:].rearrange("p (c m t) -> p c t m", c=MID_PASSES, t=PACK)
+            )
+
+        def sort_w1(e):
+            nc.vector.tensor_copy(
+                out=w1[:, e].bitcast(I32),
+                in_=w1_raw[:, e, :].bitcast(I32).rearrange("p (c m t) -> p c t m", c=MID_PASSES, t=PACK),
             )
 
         def transpose_x(s):
-            e, first = s // STEPS_PER_GROUP, PAIR * (s % STEPS_PER_GROUP)
-            x_t = psum_xy.tile([P, PAIR, 2, P], F32, tag="xy")
-            for j in range(PAIR):
-                words = x_sb[:, e, first + j, :].bitcast(F32)
-                for u in range(2):
-                    nc.tensor.transpose(out=x_t[:, j, u, :], in_=words[:, u : HID // 2 : 2], identity=ident_f32[:])
-            x_grouped[s] = work.tile([P, PAIR * P * PACK], BF16, align_bytes=64, name="x_grouped")
-            nc.scalar.copy(
-                out=x_grouped[s][:].bitcast(F32).rearrange("p (j r u) -> p j r u", j=PAIR, u=2),
-                in_=x_t[:].rearrange("p j u r -> p j r u"),
-            )
+            e, first = s // STEPS_PER_GROUP, QUAD * (s % STEPS_PER_GROUP)
+            x_grouped[s] = work.tile([P, TOK * PACK], BF16, align_bytes=64, name="x_grouped")
+            for h in range(QUAD // 2):
+                x_t = psum_x.tile([P, 2, 2, P], F32, tag="x")
+                for j in range(2):
+                    words = x_sb[:, e, first + 2 * h + j, :].bitcast(F32)
+                    for u in range(2):
+                        nc.tensor.transpose(out=x_t[:, j, u, :], in_=words[:, u : HID // 2 : 2], identity=ident_f32[:])
+                half = TOK * PACK // 2
+                nc.scalar.copy(
+                    out=x_grouped[s][:, half * h : half * (h + 1)].bitcast(F32).rearrange("p (j r u) -> p j r u", j=2, u=2),
+                    in_=x_t[:].rearrange("p j u r -> p j r u"),
+                )
 
         def quantise_x(s):
-            nc.vector.quantize_mx(
-                out=x_codes[:, s].rearrange("p j r -> p (j r)").bitcast(FP8X4),
-                scales=x_scales[:, s].rearrange("p j r -> p (j r)"),
-                in_=x_grouped[s][:],
-            )
+            x_codes[s] = work.tile([P, TOK], U32, align_bytes=64, name="x_codes")
+            x_scales[s] = work.tile([P, TOK], U8, align_bytes=64, name="x_scales")
+            nc.vector.quantize_mx(out=x_codes[s][:].bitcast(FP8X4), scales=x_scales[s][:], in_=x_grouped[s][:])
 
-        def layer1(s):
+        def layer1(s, c, t):
             e = s // STEPS_PER_GROUP
-            for j in range(PAIR):
-                for c in range(MID_PASSES):
-                    columns = slice(K_PASS * c, K_PASS * (c + 1))
-                    y_ps = psum_xy.tile([P, K_PASS], F32, tag="xy")
-                    nc.tensor.matmul_mx(
-                        out=y_ps[:],
-                        lhsT=x_codes[:, s, j, :].bitcast(FP8X4),
-                        lhsT_scale=x_scales[:, s, j, :],
-                        rhs=w1[:, e, columns].bitcast(FP8X4),
-                        rhs_scale=w1_scales[4 * e : P, columns],
-                        start=True,
-                        stop=True,
-                    )
-                    y_sorted[s, j, c] = work.tile([P, PACK, P], BF16, name="y_sorted", bufs=Y_SORTED_BUFS)
-                    nc.vector.tensor_tensor(
-                        out=y_sorted[s, j, c][:],
-                        in0=y_ps[:].rearrange("q (p t) -> q t p", t=PACK),
-                        in1=b1_sorted[:, e, c],
-                        op=ADD,
-                    )
-
-        def transpose_y(s):
-            y_grouped[s] = work.tile([P, PAIR, MID_PASSES, P, PACK], BF16, align_bytes=64, name="y_grouped")
-            for j in range(PAIR):
-                y_t = psum_yt.tile([P, MID_PASSES, PACK, P], BF16)
-                for c in range(MID_PASSES):
-                    for t in range(PACK):
-                        nc.tensor.transpose(out=y_t[:, c, t, :], in_=y_sorted[s, j, c][:, t, :], identity=ident_bf16[:])
-                nc.scalar.copy(out=y_grouped[s][:, j], in_=y_t[:].rearrange("p c t r -> p c r t"))
-
-        def quantise_y(s):
-            y_codes[s] = work.tile([P, PAIR, MID_PASSES, P], U32, align_bytes=64, name="y_codes")
-            y_scales[s] = work.tile([P, PAIR, MID_PASSES, P], U8, align_bytes=64, name="y_scales")
-            nc.vector.quantize_mx(
-                out=y_codes[s][:].rearrange("p j c r -> p (j c r)").bitcast(FP8X4),
-                scales=y_scales[s][:].rearrange("p j c r -> p (j c r)"),
-                in_=y_grouped[s][:].rearrange("p j c r t -> p (j c r t)"),
+            if t == 0:
+                y_plain[s, c] = work.tile([P, PACK, TOK], BF16, align_bytes=64, name="y_plain", bufs=4)
+            y_ps = psum_y.tile([P, TOK], F32, tag="y")
+            nc.tensor.matmul_mx(
+                out=y_ps[:],
+                lhsT=w1[:, e, c, t, :].bitcast(FP8X4),
+                lhsT_scale=w1_scales[4 * e : P, c, t, :],
+                rhs=x_codes[s][:].bitcast(FP8X4),
+                rhs_scale=x_scales[s][:],
+                start=True,
+                stop=True,
+            )
+            column = MID_PASSES * e + c
+            nc.scalar.activation(
+                out=y_plain[s, c][:, t, :], in_=y_ps[:], func=IDENTITY, bias=b1[:, column, t : t + 1], scale=1.0
             )
 
-        def layer2(s):
-            e, first = s // STEPS_PER_GROUP, PAIR * (s % STEPS_PER_GROUP)
-            o_sb = work.tile([P, PAIR, HID], F32, bufs=3)
-            for j in range(PAIR):
-                o_ps = psum_o.tile([P, HID], F32)
-                for c in range(MID_PASSES):
-                    nc.tensor.matmul_mx(
-                        out=o_ps[:],
-                        lhsT=y_codes[s][:, j, c, :].bitcast(FP8X4),
-                        lhsT_scale=y_scales[s][:, j, c, :],
-                        rhs=w2[:, e, c, :].bitcast(FP8X4),
-                        rhs_scale=w2_scales[4 * e : P, c, :],
-                        start=(c == 0),
-                        stop=(c == MID_PASSES - 1),
-                    )
-                nc.vector.tensor_tensor(out=o_sb[:, j, :], in0=o_ps[:], in1=b2_rows[:, e, :], op=ADD)
-            nc.sync.dma_start(out=out_tiles[e][:, first : first + PAIR, :], in_=o_sb[:])
+        def group_y(s, c):
+            y_grouped[s, c] = work.tile([P, TOK, PACK], BF16, align_bytes=64, name="y_grouped", bufs=4)
+            nc.vector.tensor_copy(out=y_grouped[s, c][:], in_=y_plain[s, c][:].rearrange("p t n -> p n t"))
 
-        for r in range(-LAYER1_TO_Y - X_TO_LAYER1, STEPS + Y_TO_LAYER2):
-            x_step = r + LAYER1_TO_Y + X_TO_LAYER1
-            layer1_step = r + LAYER1_TO_Y
-            layer2_step = r - Y_TO_LAYER2
-            if x_step < STEPS:
-                if x_step % STEPS_PER_GROUP == 0:
-                    sort_b1(x_step // STEPS_PER_GROUP)
+        def quantise_y(s, c):
+            y_codes[s, c] = work.tile([P, TOK], U32, align_bytes=64, name="y_codes", bufs=4)
+            y_scales[s, c] = work.tile([P, TOK], U8, align_bytes=64, name="y_scales", bufs=4)
+            nc.vector.quantize_mx(
+                out=y_codes[s, c][:].bitcast(FP8X4),
+                scales=y_scales[s, c][:],
+                in_=y_grouped[s, c][:].rearrange("p n t -> p (n t)"),
+            )
+
+        def layer2(s, j):
+            e = s // STEPS_PER_GROUP
+            o_ps[s, j] = psum_o.tile([P, HID], F32, tag="o", name="o_ps")
+            for c in range(MID_PASSES):
+                nc.tensor.matmul_mx(
+                    out=o_ps[s, j][:],
+                    lhsT=y_codes[s, c][:, P * j : P * (j + 1)].bitcast(FP8X4),
+                    lhsT_scale=y_scales[s, c][:, P * j : P * (j + 1)],
+                    rhs=w2[:, e, c, :].bitcast(FP8X4),
+                    rhs_scale=w2_scales[4 * e : P, c, :],
+                    start=(c == 0),
+                    stop=(c == MID_PASSES - 1),
+                )
+
+        def finish(s, j):
+            e, first = s // STEPS_PER_GROUP, QUAD * (s % STEPS_PER_GROUP)
+            if j % 2 == 0:
+                o_sb[s, j // 2] = work.tile([P, 2, HID], F32, name="o_sb", bufs=6)
+            nc.vector.tensor_tensor(out=o_sb[s, j // 2][:, j % 2, :], in0=o_ps[s, j][:], in1=b2_rows[:, e, :], op=ADD)
+            if j % 2 == 1:
+                nc.sync.dma_start(out=out_tiles[e][:, first + j - 1 : first + j + 1, :], in_=o_sb[s, j // 2][:])
+
+        sort_w1_scales()
+        sort_w1(0)
+        nc.gpsimd.tensor_copy(out=b1[:], in_=b1_raw[:])
+        for k in range(-2, STEPS + 1):
+            x_step, l1_step, y_step, o_step = k + 2, k + 1, k, k - 1
+            has_x = x_step < STEPS
+            has_l1 = 0 <= l1_step < STEPS
+            has_y = 0 <= y_step < STEPS
+            has_o = 0 <= o_step
+            if has_x:
                 transpose_x(x_step)
-            if 0 <= r < STEPS:
-                transpose_y(r)
-            if 0 <= layer1_step < STEPS:
-                layer1(layer1_step)
-            if x_step < STEPS:
-                quantise_x(x_step)
-            if 0 <= r < STEPS:
-                quantise_y(r)
-            if 0 <= layer2_step:
-                layer2(layer2_step)
+            for j in range(QUAD):
+                if has_l1:
+                    for i in (2 * j, 2 * j + 1):
+                        layer1(l1_step, i // PACK, i % PACK)
+                if has_o:
+                    layer2(o_step, j)
+                if j == 0 and has_y:
+                    if k % STEPS_PER_GROUP == 0 and k // STEPS_PER_GROUP + 1 < GROUPS:
+                        sort_w1(k // STEPS_PER_GROUP + 1)
+                    group_y(y_step, 0)
+                if j == 1 and has_y:
+                    group_y(y_step, 1)
+                if j == 2 and has_y:
+                    quantise_y(y_step, 0)
+                if has_o:
+                    finish(o_step, j)
+                if j == 1 and has_x:
+                    quantise_x(x_step)
+                if j == 2 and has_y:
+                    quantise_y(y_step, 1)

@@ -20,10 +20,11 @@ HID = 512
 MID = 1024
 MID_PASSES = MID // K_PASS
 TILES = 1024 // P
-QUAD = 4
-TOK = QUAD * P
-STEPS = GROUPS * TILES // QUAD
-STEPS_PER_GROUP = TILES // QUAD
+STEP_TILES = ((2, 2, 4), (4, 4), (4, 4), (4, 2, 2))
+STEP_LIST = [(e, sum(widths[:i]), w) for e, widths in enumerate(STEP_TILES) for i, w in enumerate(widths)]
+STEPS = len(STEP_LIST)
+
+RUN = 4
 
 FLOPS = 2 * GROUPS * 1024 * (HID * MID + MID * HID)
 
@@ -62,9 +63,11 @@ def tile_dummytemodel_pa_t_e_kernel(
         def load_tokens(e, first, count):
             nc.sync.dma_start(out=x_sb[:, e, first : first + count, :], in_=hf_tiles[e][:, first : first + count, :])
 
-        def load_w1(e):
+        def load_w1(e, first, count):
+            columns = slice(K_PASS * first, K_PASS * (first + count))
             nc.sync.dma_start(
-                out=w1_raw[:, e, :].bitcast(I32), in_=g1_w_words[e].rearrange("p n t -> p (n t)").bitcast(I32)
+                out=w1_raw[:, e, columns].bitcast(I32),
+                in_=g1_w_words[e][:, columns, :].rearrange("p n t -> p (n t)").bitcast(I32),
             )
 
         def load_w2(e):
@@ -73,17 +76,18 @@ def tile_dummytemodel_pa_t_e_kernel(
                 in_=g2_w_words[MID_PASSES * e : MID_PASSES * (e + 1)].rearrange("c p n t -> p c (n t)").bitcast(I32),
             )
 
-        for first in range(0, QUAD, 2):
-            load_tokens(0, first, 2)
+        load_tokens(0, 0, 2)
         for quadrant in range(4):
             rows = slice(4 * quadrant, 4 * quadrant + 4)
             nc.sync.dma_start(
                 out=w1_scales_raw[32 * quadrant : 32 * quadrant + 16, :].bitcast(I32),
                 in_=g1_w_scales[:, rows, :].bitcast(I32),
             )
-        load_w1(0)
+        load_w1(0, 0, 1)
+        load_w1(0, 1, 1)
         nc.sync.dma_start(out=b1_raw[:], in_=g1_b.rearrange("e (c p t) -> p (e c) t", c=MID_PASSES, t=PACK))
-        load_tokens(0, QUAD, QUAD)
+        load_tokens(0, 2, 2)
+        load_tokens(0, 4, 4)
         for c in range(MID_PASSES):
             for quadrant in range(4):
                 rows = slice(4 * quadrant, 4 * quadrant + 4)
@@ -92,14 +96,14 @@ def tile_dummytemodel_pa_t_e_kernel(
                     in_=g2_w_scales[c : GROUPS * MID_PASSES : MID_PASSES, rows, :].bitcast(I32),
                 )
         load_w2(0)
-        load_w1(1)
+        load_w1(1, 0, MID_PASSES)
+        load_tokens(1, 0, TILES)
         nc.sync.dma_start(
             out=b2_rows[:].rearrange("q e n -> q (e n)"), in_=g2_b.rearrange("e n -> (e n)").partition_broadcast(P)
         )
-        load_tokens(1, 0, TILES)
         load_w2(1)
         for e in range(2, GROUPS):
-            load_w1(e)
+            load_w1(e, 0, MID_PASSES)
             load_tokens(e, 0, TILES)
             load_w2(e)
 
@@ -118,37 +122,41 @@ def tile_dummytemodel_pa_t_e_kernel(
                 out=w1_scales[:], in_=w1_scales_raw[:].rearrange("p (c m t) -> p c t m", c=MID_PASSES, t=PACK)
             )
 
-        def sort_w1(e):
+        def sort_w1(e, first, count):
             nc.vector.tensor_copy(
-                out=w1[:, e].bitcast(I32),
-                in_=w1_raw[:, e, :].bitcast(I32).rearrange("p (c m t) -> p c t m", c=MID_PASSES, t=PACK),
+                out=w1[:, e, first : first + count].bitcast(I32),
+                in_=w1_raw[:, e, K_PASS * first : K_PASS * (first + count)]
+                .bitcast(I32)
+                .rearrange("p (c m t) -> p c t m", c=count, t=PACK),
             )
 
         def transpose_x(s):
-            e, first = s // STEPS_PER_GROUP, QUAD * (s % STEPS_PER_GROUP)
-            x_grouped[s] = work.tile([P, TOK * PACK], BF16, align_bytes=64, name="x_grouped")
-            for h in range(QUAD // 2):
+            e, first, tiles = STEP_LIST[s]
+            x_grouped[s] = work.tile([P, tiles * P * PACK], BF16, align_bytes=64, name="x_grouped")
+            for h in range(tiles // 2):
                 x_t = psum_x.tile([P, 2, 2, P], F32, tag="x")
                 for j in range(2):
                     words = x_sb[:, e, first + 2 * h + j, :].bitcast(F32)
                     for u in range(2):
                         nc.tensor.transpose(out=x_t[:, j, u, :], in_=words[:, u : HID // 2 : 2], identity=ident_f32[:])
-                half = TOK * PACK // 2
+                half = 2 * P * PACK
                 nc.scalar.copy(
                     out=x_grouped[s][:, half * h : half * (h + 1)].bitcast(F32).rearrange("p (j r u) -> p j r u", j=2, u=2),
                     in_=x_t[:].rearrange("p j u r -> p j r u"),
                 )
 
         def quantise_x(s):
-            x_codes[s] = work.tile([P, TOK], U32, align_bytes=64, name="x_codes")
-            x_scales[s] = work.tile([P, TOK], U8, align_bytes=64, name="x_scales")
+            tokens = STEP_LIST[s][2] * P
+            x_codes[s] = work.tile([P, tokens], U32, align_bytes=64, name="x_codes")
+            x_scales[s] = work.tile([P, tokens], U8, align_bytes=64, name="x_scales")
             nc.vector.quantize_mx(out=x_codes[s][:].bitcast(FP8X4), scales=x_scales[s][:], in_=x_grouped[s][:])
 
         def layer1(s, c, t):
-            e = s // STEPS_PER_GROUP
+            e, first, tiles = STEP_LIST[s]
+            tokens = tiles * P
             if t == 0:
-                y_plain[s, c] = work.tile([P, PACK, TOK], BF16, align_bytes=64, name="y_plain", bufs=4)
-            y_ps = psum_y.tile([P, TOK], F32, tag="y")
+                y_plain[s, c] = work.tile([P, PACK, tokens], BF16, align_bytes=64, name="y_plain", bufs=4)
+            y_ps = psum_y.tile([P, tokens], F32, tag="y")
             nc.tensor.matmul_mx(
                 out=y_ps[:],
                 lhsT=w1[:, e, c, t, :].bitcast(FP8X4),
@@ -164,12 +172,17 @@ def tile_dummytemodel_pa_t_e_kernel(
             )
 
         def group_y(s, c):
-            y_grouped[s, c] = work.tile([P, TOK, PACK], BF16, align_bytes=64, name="y_grouped", bufs=4)
-            nc.vector.tensor_copy(out=y_grouped[s, c][:], in_=y_plain[s, c][:].rearrange("p t n -> p n t"))
+            tokens = STEP_LIST[s][2] * P
+            y_grouped[s, c] = work.tile([P, tokens, PACK], BF16, align_bytes=64, name="y_grouped", bufs=4)
+            nc.vector.tensor_copy(
+                out=y_grouped[s, c][:].rearrange("p (k i) t -> p k t i", i=RUN),
+                in_=y_plain[s, c][:].rearrange("p t (k i) -> p k t i", i=RUN),
+            )
 
         def quantise_y(s, c):
-            y_codes[s, c] = work.tile([P, TOK], U32, align_bytes=64, name="y_codes", bufs=4)
-            y_scales[s, c] = work.tile([P, TOK], U8, align_bytes=64, name="y_scales", bufs=4)
+            tokens = STEP_LIST[s][2] * P
+            y_codes[s, c] = work.tile([P, tokens], U32, align_bytes=64, name="y_codes", bufs=4)
+            y_scales[s, c] = work.tile([P, tokens], U8, align_bytes=64, name="y_scales", bufs=4)
             nc.vector.quantize_mx(
                 out=y_codes[s, c][:].bitcast(FP8X4),
                 scales=y_scales[s, c][:],
@@ -177,7 +190,7 @@ def tile_dummytemodel_pa_t_e_kernel(
             )
 
         def layer2(s, j):
-            e = s // STEPS_PER_GROUP
+            e = STEP_LIST[s][0]
             o_ps[s, j] = psum_o.tile([P, HID], F32, tag="o", name="o_ps")
             for c in range(MID_PASSES):
                 nc.tensor.matmul_mx(
@@ -191,7 +204,7 @@ def tile_dummytemodel_pa_t_e_kernel(
                 )
 
         def finish(s, j):
-            e, first = s // STEPS_PER_GROUP, QUAD * (s % STEPS_PER_GROUP)
+            e, first, tiles = STEP_LIST[s]
             if j % 2 == 0:
                 o_sb[s, j // 2] = work.tile([P, 2, HID], F32, name="o_sb", bufs=6)
             nc.vector.tensor_tensor(out=o_sb[s, j // 2][:, j % 2, :], in0=o_ps[s, j][:], in1=b2_rows[:, e, :], op=ADD)
@@ -199,33 +212,33 @@ def tile_dummytemodel_pa_t_e_kernel(
                 nc.sync.dma_start(out=out_tiles[e][:, first + j - 1 : first + j + 1, :], in_=o_sb[s, j // 2][:])
 
         sort_w1_scales()
-        sort_w1(0)
+        sort_w1(0, 0, 1)
         nc.gpsimd.tensor_copy(out=b1[:], in_=b1_raw[:])
         for k in range(-2, STEPS + 1):
             x_step, l1_step, y_step, o_step = k + 2, k + 1, k, k - 1
             has_x = x_step < STEPS
             has_l1 = 0 <= l1_step < STEPS
             has_y = 0 <= y_step < STEPS
-            has_o = 0 <= o_step
-            if has_x:
-                transpose_x(x_step)
-            for j in range(QUAD):
+            o_tiles = STEP_LIST[o_step][2] if 0 <= o_step else 0
+            for j in range(4):
+                if j == 2 - 2 * (k < -1) and has_x:
+                    transpose_x(x_step)
                 if has_l1:
                     for i in (2 * j, 2 * j + 1):
                         layer1(l1_step, i // PACK, i % PACK)
-                if has_o:
+                if j < o_tiles:
                     layer2(o_step, j)
-                if j == 0 and has_y:
-                    if k % STEPS_PER_GROUP == 0 and k // STEPS_PER_GROUP + 1 < GROUPS:
-                        sort_w1(k // STEPS_PER_GROUP + 1)
-                    group_y(y_step, 0)
-                if j == 1 and has_y:
-                    group_y(y_step, 1)
+                if j == 0 and has_x and STEP_LIST[x_step][1] == 0 and x_step > 0:
+                    sort_w1(STEP_LIST[x_step][0], 0, MID_PASSES)
+                if j < 2 and has_y:
+                    group_y(y_step, j)
                 if j == 2 and has_y:
                     quantise_y(y_step, 0)
-                if has_o:
-                    finish(o_step, j)
-                if j == 1 and has_x:
+                if j == 2 and has_x:
                     quantise_x(x_step)
-                if j == 2 and has_y:
+                    if x_step == 0:
+                        sort_w1(0, 1, 1)
+                if j == 3 and has_y:
                     quantise_y(y_step, 1)
+                if j < o_tiles:
+                    finish(o_step, j)

@@ -76,36 +76,53 @@ def tile_dummytemodel_pa_t_e_kernel(
                 in_=g2_w_words[MID_PASSES * e : MID_PASSES * (e + 1)].rearrange("c p n t -> p c (n t)").bitcast(I32),
             )
 
-        load_tokens(0, 0, 2)
-        for quadrant in range(4):
-            rows = slice(4 * quadrant, 4 * quadrant + 4)
-            nc.sync.dma_start(
-                out=w1_scales_raw[32 * quadrant : 32 * quadrant + 16, :].bitcast(I32),
-                in_=g1_w_scales[:, rows, :].bitcast(I32),
-            )
-        load_w1(0, 0, 1)
-        load_w1(0, 1, 1)
-        nc.sync.dma_start(out=b1_raw[:], in_=g1_b.rearrange("e (c p t) -> p (e c) t", c=MID_PASSES, t=PACK))
-        load_tokens(0, 2, 2)
-        load_tokens(0, 4, 4)
-        for c in range(MID_PASSES):
+        def load_w1_scales():
             for quadrant in range(4):
                 rows = slice(4 * quadrant, 4 * quadrant + 4)
                 nc.sync.dma_start(
-                    out=w2_scales[32 * quadrant : 32 * quadrant + 16, c, :].bitcast(I32),
-                    in_=g2_w_scales[c : GROUPS * MID_PASSES : MID_PASSES, rows, :].bitcast(I32),
+                    out=w1_scales_raw[32 * quadrant : 32 * quadrant + 16, :].bitcast(I32),
+                    in_=g1_w_scales[:, rows, :].bitcast(I32),
                 )
+
+        def load_w2_scales():
+            for c in range(MID_PASSES):
+                for quadrant in range(4):
+                    rows = slice(4 * quadrant, 4 * quadrant + 4)
+                    nc.sync.dma_start(
+                        out=w2_scales[32 * quadrant : 32 * quadrant + 16, c, :].bitcast(I32),
+                        in_=g2_w_scales[c : GROUPS * MID_PASSES : MID_PASSES, rows, :].bitcast(I32),
+                    )
+
+        def load_b1():
+            nc.scalar.dma_start(out=b1_raw[:], in_=g1_b.rearrange("e (c p t) -> p (e c) t", c=MID_PASSES, t=PACK))
+
+        def load_b2(e):
+            nc.sync.dma_start(out=b2_rows[:, e, :], in_=g2_b[e].partition_broadcast(P))
+
+        def load_b2_all():
+            nc.sync.dma_start(
+                out=b2_rows[:].rearrange("q e n -> q (e n)"), in_=g2_b.rearrange("e n -> (e n)").partition_broadcast(P)
+            )
+
+        load_tokens(0, 0, 2)
+        load_b1()
+        load_w1_scales()
+        load_w1(0, 0, 1)
+        load_w1(0, 1, 1)
+        load_tokens(0, 2, 6)
         load_w2(0)
+        load_w2_scales()
+        load_tokens(1, 0, 4)
         load_w1(1, 0, MID_PASSES)
-        load_tokens(1, 0, TILES)
-        nc.sync.dma_start(
-            out=b2_rows[:].rearrange("q e n -> q (e n)"), in_=g2_b.rearrange("e n -> (e n)").partition_broadcast(P)
-        )
+        load_b2_all()
+        load_tokens(1, 4, 4)
         load_w2(1)
-        for e in range(2, GROUPS):
-            load_w1(e, 0, MID_PASSES)
-            load_tokens(e, 0, TILES)
-            load_w2(e)
+        load_w1(2, 0, MID_PASSES)
+        load_tokens(2, 0, TILES)
+        load_w2(2)
+        load_w1(3, 0, MID_PASSES)
+        load_tokens(3, 0, TILES)
+        load_w2(3)
 
         x_grouped = {}
         x_codes = {}
@@ -117,9 +134,10 @@ def tile_dummytemodel_pa_t_e_kernel(
         o_sb = {}
         o_ps = {}
 
-        def sort_w1_scales():
+        def sort_w1_scales(c):
             nc.vector.tensor_copy(
-                out=w1_scales[:], in_=w1_scales_raw[:].rearrange("p (c m t) -> p c t m", c=MID_PASSES, t=PACK)
+                out=w1_scales[:, c],
+                in_=w1_scales_raw[:, K_PASS * c : K_PASS * (c + 1)].rearrange("p (m t) -> p t m", t=PACK),
             )
 
         def sort_w1(e, first, count):
@@ -132,23 +150,26 @@ def tile_dummytemodel_pa_t_e_kernel(
 
         def transpose_x(s):
             e, first, tiles = STEP_LIST[s]
-            x_grouped[s] = work.tile([P, tiles * P * PACK], BF16, align_bytes=64, name="x_grouped")
-            for h in range(tiles // 2):
-                x_t = psum_x.tile([P, 2, 2, P], F32, tag="x")
-                for j in range(2):
-                    words = x_sb[:, e, first + 2 * h + j, :].bitcast(F32)
+            x_grouped[s] = work.tile([P, tiles * P * PACK], BF16, align_bytes=64, name="x_grouped", bufs=2)
+            for h in range(0, tiles, 2):
+                pair = min(2, tiles - h)
+                x_t = psum_x.tile([P, pair, 2, P], F32, tag="x")
+                for j in range(pair):
+                    words = x_sb[:, e, first + h + j, :].bitcast(F32)
                     for u in range(2):
                         nc.tensor.transpose(out=x_t[:, j, u, :], in_=words[:, u : HID // 2 : 2], identity=ident_f32[:])
-                half = 2 * P * PACK
-                nc.scalar.copy(
-                    out=x_grouped[s][:, half * h : half * (h + 1)].bitcast(F32).rearrange("p (j r u) -> p j r u", j=2, u=2),
+                copy_x = nc.scalar.copy
+                copy_x(
+                    out=x_grouped[s][:, K_PASS * h : K_PASS * (h + pair)]
+                    .bitcast(F32)
+                    .rearrange("p (j r u) -> p j r u", j=pair, u=2),
                     in_=x_t[:].rearrange("p j u r -> p j r u"),
                 )
 
         def quantise_x(s):
             tokens = STEP_LIST[s][2] * P
-            x_codes[s] = work.tile([P, tokens], U32, align_bytes=64, name="x_codes")
-            x_scales[s] = work.tile([P, tokens], U8, align_bytes=64, name="x_scales")
+            x_codes[s] = work.tile([P, tokens], U32, align_bytes=64, name="x_codes", bufs=3)
+            x_scales[s] = work.tile([P, tokens], U8, align_bytes=64, name="x_scales", bufs=3)
             nc.vector.quantize_mx(out=x_codes[s][:].bitcast(FP8X4), scales=x_scales[s][:], in_=x_grouped[s][:])
 
         def layer1(s, c, t):
@@ -174,10 +195,13 @@ def tile_dummytemodel_pa_t_e_kernel(
         def group_y(s, c):
             tokens = STEP_LIST[s][2] * P
             y_grouped[s, c] = work.tile([P, tokens, PACK], BF16, align_bytes=64, name="y_grouped", bufs=4)
-            nc.vector.tensor_copy(
-                out=y_grouped[s, c][:].rearrange("p (k i) t -> p k t i", i=RUN),
-                in_=y_plain[s, c][:].rearrange("p t (k i) -> p k t i", i=RUN),
-            )
+            dst = y_grouped[s, c][:].rearrange("p (k i) t -> p k t i", i=RUN)
+            src = y_plain[s, c][:].rearrange("p t (k i) -> p k t i", i=RUN)
+            blocks = tokens // RUN
+            a = blocks * 24 // 32 if s >= 5 else blocks
+            nc.vector.tensor_copy(out=dst[:, :a], in_=src[:, :a])
+            if a < blocks:
+                nc.scalar.copy(out=dst[:, a:], in_=src[:, a:])
 
         def quantise_y(s, c):
             tokens = STEP_LIST[s][2] * P
@@ -205,39 +229,43 @@ def tile_dummytemodel_pa_t_e_kernel(
 
         def finish(s, j):
             e, first, tiles = STEP_LIST[s]
-            if j % 2 == 0:
-                o_sb[s, j // 2] = work.tile([P, 2, HID], F32, name="o_sb", bufs=6)
-            nc.vector.tensor_tensor(out=o_sb[s, j // 2][:, j % 2, :], in0=o_ps[s, j][:], in1=b2_rows[:, e, :], op=ADD)
-            if j % 2 == 1:
-                nc.sync.dma_start(out=out_tiles[e][:, first + j - 1 : first + j + 1, :], in_=o_sb[s, j // 2][:])
+            pair = min(2, tiles)
+            if j % pair == 0:
+                o_sb[s] = work.tile([P, pair, HID], F32, name="o_sb", bufs=6)
+            nc.vector.tensor_tensor(out=o_sb[s][:, j % pair, :], in0=o_ps[s, j][:], in1=b2_rows[:, e, :], op=ADD)
+            if j % pair == pair - 1:
+                nc.sync.dma_start(out=out_tiles[e][:, first + j - pair + 1 : first + j + 1, :], in_=o_sb[s][:])
 
-        sort_w1_scales()
+        sort_w1_scales(0)
         sort_w1(0, 0, 1)
         nc.gpsimd.tensor_copy(out=b1[:], in_=b1_raw[:])
-        for k in range(-2, STEPS + 1):
+        for s in range(2 - 1):
+            transpose_x(s)
+            quantise_x(s)
+        sort_w1_scales(1)
+        sort_w1(0, 1, 1)
+        for k in range(-1, STEPS + 1):
             x_step, l1_step, y_step, o_step = k + 2, k + 1, k, k - 1
             has_x = x_step < STEPS
-            has_l1 = 0 <= l1_step < STEPS
+            has_l1 = l1_step < STEPS
             has_y = 0 <= y_step < STEPS
             o_tiles = STEP_LIST[o_step][2] if 0 <= o_step else 0
             for j in range(4):
-                if j == 2 - 2 * (k < -1) and has_x:
+                if j == 2 and has_x:
                     transpose_x(x_step)
                 if has_l1:
                     for i in (2 * j, 2 * j + 1):
                         layer1(l1_step, i // PACK, i % PACK)
                 if j < o_tiles:
                     layer2(o_step, j)
-                if j == 0 and has_x and STEP_LIST[x_step][1] == 0 and x_step > 0:
-                    sort_w1(STEP_LIST[x_step][0], 0, MID_PASSES)
+                if j == 0 and l1_step + 1 < STEPS and STEP_LIST[l1_step + 1][1] == 0:
+                    sort_w1(STEP_LIST[l1_step + 1][0], 0, MID_PASSES)
                 if j < 2 and has_y:
                     group_y(y_step, j)
                 if j == 2 and has_y:
                     quantise_y(y_step, 0)
                 if j == 2 and has_x:
                     quantise_x(x_step)
-                    if x_step == 0:
-                        sort_w1(0, 1, 1)
                 if j == 3 and has_y:
                     quantise_y(y_step, 1)
                 if j < o_tiles:

@@ -106,13 +106,14 @@ def tile_dummytemodel_pa_t_e_kernel(
 
         load_tokens(0, 0, 2)
         load_b1()
+        load_tokens(0, 2, 2)
         load_w1_scales()
         load_w1(0, 0, 1)
         load_w1(0, 1, 1)
-        load_tokens(0, 2, 6)
+        load_tokens(0, 4, 4)
         load_w2(0)
-        load_w2_scales()
         load_tokens(1, 0, 4)
+        load_w2_scales()
         load_w1(1, 0, MID_PASSES)
         load_b2_all()
         load_tokens(1, 4, 4)
@@ -229,7 +230,7 @@ def tile_dummytemodel_pa_t_e_kernel(
 
         def finish(s, j):
             e, first, tiles = STEP_LIST[s]
-            pair = min(2, tiles)
+            pair = 1 if s == STEPS - 1 else min(2, tiles)
             if j % pair == 0:
                 o_sb[s] = work.tile([P, pair, HID], F32, name="o_sb", bufs=6)
             nc.vector.tensor_tensor(out=o_sb[s][:, j % pair, :], in0=o_ps[s, j][:], in1=b2_rows[:, e, :], op=ADD)
@@ -239,19 +240,20 @@ def tile_dummytemodel_pa_t_e_kernel(
         sort_w1_scales(0)
         sort_w1(0, 0, 1)
         nc.gpsimd.tensor_copy(out=b1[:], in_=b1_raw[:])
-        for s in range(2 - 1):
-            transpose_x(s)
-            quantise_x(s)
+        transpose_x(0)
+        quantise_x(0)
+        transpose_x(1)
+        quantise_x(1)
         sort_w1_scales(1)
         sort_w1(0, 1, 1)
         for k in range(-1, STEPS + 1):
             x_step, l1_step, y_step, o_step = k + 2, k + 1, k, k - 1
-            has_x = x_step < STEPS
+            has_x = 1 < x_step < STEPS
             has_l1 = l1_step < STEPS
             has_y = 0 <= y_step < STEPS
             o_tiles = STEP_LIST[o_step][2] if 0 <= o_step else 0
             for j in range(4):
-                if j == 2 and has_x:
+                if j == 0 and has_x:
                     transpose_x(x_step)
                 if has_l1:
                     for i in (2 * j, 2 * j + 1):

@@ -24,6 +24,7 @@ STEP_TILES = ((2, 2, 4), (4, 4), (4, 4), (4, 2, 2))
 STEP_LIST = [(e, sum(widths[:i]), w) for e, widths in enumerate(STEP_TILES) for i, w in enumerate(widths)]
 STEPS = len(STEP_LIST)
 
+WARM_UP = 4
 RUN = 4
 
 FLOPS = 2 * GROUPS * 1024 * (HID * MID + MID * HID)
@@ -59,6 +60,12 @@ def tile_dummytemodel_pa_t_e_kernel(
         nc.vector.memset(w1_scales_raw[:].bitcast(I32), 0)
         nc.vector.memset(w2_scales[:].bitcast(I32), 0)
         make_identity(nc, ident_f32[:])
+
+        zeros = keep.tile([P, HID], BF16)
+        nc.vector.memset(zeros[:], 0.0)
+        idle_ps = psum_o.tile([P, HID], F32, tag="o", name="o_ps")
+        for i in range(WARM_UP):
+            nc.tensor.matmul(out=idle_ps[:], lhsT=zeros[:, :P], rhs=zeros[:], start=True, stop=True)
 
         def load_tokens(e, first, count):
             nc.sync.dma_start(out=x_sb[:, e, first : first + count, :], in_=hf_tiles[e][:, first : first + count, :])
@@ -199,10 +206,11 @@ def tile_dummytemodel_pa_t_e_kernel(
             dst = y_grouped[s, c][:].rearrange("p (k i) t -> p k t i", i=RUN)
             src = y_plain[s, c][:].rearrange("p t (k i) -> p k t i", i=RUN)
             blocks = tokens // RUN
-            a = blocks * 24 // 32 if s >= 5 else blocks
-            nc.vector.tensor_copy(out=dst[:, :a], in_=src[:, :a])
-            if a < blocks:
-                nc.scalar.copy(out=dst[:, a:], in_=src[:, a:])
+            share = 16 if s >= 8 else 8 if s >= 5 else 0
+            scalar_from = blocks - blocks * share // 32
+            nc.vector.tensor_copy(out=dst[:, :scalar_from], in_=src[:, :scalar_from])
+            if scalar_from < blocks:
+                nc.scalar.copy(out=dst[:, scalar_from:], in_=src[:, scalar_from:])
 
         def quantise_y(s, c):
             tokens = STEP_LIST[s][2] * P
@@ -216,7 +224,10 @@ def tile_dummytemodel_pa_t_e_kernel(
 
         def layer2(s, j):
             e = STEP_LIST[s][0]
-            o_ps[s, j] = psum_o.tile([P, HID], F32, tag="o", name="o_ps")
+            if s == STEPS - 1:
+                o_ps[s, j] = psum_y.tile([P, HID], F32, tag="y", name="y_ps")
+            else:
+                o_ps[s, j] = psum_o.tile([P, HID], F32, tag="o", name="o_ps")
             for c in range(MID_PASSES):
                 nc.tensor.matmul_mx(
                     out=o_ps[s, j][:],
@@ -270,5 +281,8 @@ def tile_dummytemodel_pa_t_e_kernel(
                     quantise_x(x_step)
                 if j == 3 and has_y:
                     quantise_y(y_step, 1)
-                if j < o_tiles:
+                if j < o_tiles and y_step != STEPS - 1:
+                    finish(o_step, j)
+            if y_step == STEPS - 1:
+                for j in range(o_tiles):
                     finish(o_step, j)

@@ -24,7 +24,8 @@ STEP_TILES = ((2, 2, 4), (4, 4), (4, 4), (4, 2, 2))
 STEP_LIST = [(e, sum(widths[:i]), w) for e, widths in enumerate(STEP_TILES) for i, w in enumerate(widths)]
 STEPS = len(STEP_LIST)
 
-WARM_UP = 4
+WARM_UP = 3
+DIRECT_STEPS = 1
 RUN = 4
 
 FLOPS = 2 * GROUPS * 1024 * (HID * MID + MID * HID)
@@ -51,18 +52,18 @@ def tile_dummytemodel_pa_t_e_kernel(
         w2 = keep.tile([P, GROUPS, MID_PASSES, HID], U32, align_bytes=64)
         w1_scales_raw = keep.tile([P, MID], U8, align_bytes=64)
         w1_scales = keep.tile([P, MID_PASSES, PACK, P], U8, align_bytes=64)
-        w2_scales = keep.tile([P, MID_PASSES, HID], U8, align_bytes=64)
+        w2_scales = keep.tile([P, GROUPS // 2, HID], U8, align_bytes=64)
         b1_raw = keep.tile([P, GROUPS * MID_PASSES, PACK], BF16)
         b1 = keep.tile([P, GROUPS * MID_PASSES, PACK], F32)
         b2_rows = keep.tile([P, GROUPS, HID], BF16)
         ident_f32 = keep.tile([P, P], F32)
 
+        zeros = keep.tile([P, HID], BF16)
+        nc.vector.memset(zeros[:], 0.0)
         nc.vector.memset(w1_scales_raw[:].bitcast(I32), 0)
         nc.vector.memset(w2_scales[:].bitcast(I32), 0)
         make_identity(nc, ident_f32[:])
 
-        zeros = keep.tile([P, HID], BF16)
-        nc.vector.memset(zeros[:], 0.0)
         idle_ps = psum_o.tile([P, HID], F32, tag="o", name="o_ps")
         for i in range(WARM_UP):
             nc.tensor.matmul(out=idle_ps[:], lhsT=zeros[:, :P], rhs=zeros[:], start=True, stop=True)
@@ -91,17 +92,16 @@ def tile_dummytemodel_pa_t_e_kernel(
                     in_=g1_w_scales[:, rows, :].bitcast(I32),
                 )
 
-        def load_w2_scales():
-            for c in range(MID_PASSES):
-                for quadrant in range(4):
-                    rows = slice(4 * quadrant, 4 * quadrant + 4)
-                    nc.sync.dma_start(
-                        out=w2_scales[32 * quadrant : 32 * quadrant + 16, c, :].bitcast(I32),
-                        in_=g2_w_scales[c : GROUPS * MID_PASSES : MID_PASSES, rows, :].bitcast(I32),
-                    )
+        def load_w2_scales(h):
+            for quadrant in range(4):
+                rows = slice(4 * quadrant, 4 * quadrant + 4)
+                nc.sync.dma_start(
+                    out=w2_scales[32 * quadrant : 32 * quadrant + 16, h, :].bitcast(I32),
+                    in_=g2_w_scales[4 * h : 4 * h + 4, rows, :].bitcast(I32),
+                )
 
         def load_b1():
-            nc.scalar.dma_start(out=b1_raw[:], in_=g1_b.rearrange("e (c p t) -> p (e c) t", c=MID_PASSES, t=PACK))
+            nc.sync.dma_start(out=b1_raw[:], in_=g1_b.rearrange("e (c p t) -> p (e c) t", c=MID_PASSES, t=PACK))
 
         def load_b2(e):
             nc.sync.dma_start(out=b2_rows[:, e, :], in_=g2_b[e].partition_broadcast(P))
@@ -112,21 +112,22 @@ def tile_dummytemodel_pa_t_e_kernel(
             )
 
         load_tokens(0, 0, 2)
-        load_b1()
         load_tokens(0, 2, 2)
         load_w1_scales()
         load_w1(0, 0, 1)
+        load_b1()
         load_w1(0, 1, 1)
         load_tokens(0, 4, 4)
         load_w2(0)
         load_tokens(1, 0, 4)
-        load_w2_scales()
+        load_w2_scales(0)
         load_w1(1, 0, MID_PASSES)
         load_b2_all()
         load_tokens(1, 4, 4)
         load_w2(1)
         load_w1(2, 0, MID_PASSES)
         load_tokens(2, 0, TILES)
+        load_w2_scales(1)
         load_w2(2)
         load_w1(3, 0, MID_PASSES)
         load_tokens(3, 0, TILES)
@@ -200,6 +201,28 @@ def tile_dummytemodel_pa_t_e_kernel(
                 out=y_plain[s, c][:, t, :], in_=y_ps[:], func=IDENTITY, bias=b1[:, column, t : t + 1], scale=1.0
             )
 
+        def layer1_direct(s, c, j):
+            e, first, tiles = STEP_LIST[s]
+            if j == 0:
+                y_grouped[s, c] = work.tile([P, tiles * P, PACK], BF16, align_bytes=64, name="y_grouped", bufs=4)
+            y_ps = psum_y.tile([P, PACK, P], F32, tag="y")
+            for t in range(PACK):
+                nc.tensor.matmul_mx(
+                    out=y_ps[:, t, :],
+                    lhsT=w1[:, e, c, t, :].bitcast(FP8X4),
+                    lhsT_scale=w1_scales[4 * e : P, c, t, :],
+                    rhs=x_codes[s][:, P * j : P * (j + 1)].bitcast(FP8X4),
+                    rhs_scale=x_scales[s][:, P * j : P * (j + 1)],
+                    start=True,
+                    stop=True,
+                )
+            nc.vector.tensor_tensor(
+                out=y_grouped[s, c][:, P * j : P * (j + 1), :],
+                in0=y_ps[:].rearrange("p t n -> p n t"),
+                in1=b1[:, MID_PASSES * e + c, :].unsqueeze(1).to_broadcast([P, P, PACK]),
+                op=ADD,
+            )
+
         def group_y(s, c):
             tokens = STEP_LIST[s][2] * P
             y_grouped[s, c] = work.tile([P, tokens, PACK], BF16, align_bytes=64, name="y_grouped", bufs=4)
@@ -234,7 +257,7 @@ def tile_dummytemodel_pa_t_e_kernel(
                     lhsT=y_codes[s, c][:, P * j : P * (j + 1)].bitcast(FP8X4),
                     lhsT_scale=y_scales[s, c][:, P * j : P * (j + 1)],
                     rhs=w2[:, e, c, :].bitcast(FP8X4),
-                    rhs_scale=w2_scales[4 * e : P, c, :],
+                    rhs_scale=w2_scales[4 * (MID_PASSES * (e % 2) + c) : P, e // 2, :],
                     start=(c == 0),
                     stop=(c == MID_PASSES - 1),
                 )
@@ -253,10 +276,10 @@ def tile_dummytemodel_pa_t_e_kernel(
         nc.gpsimd.tensor_copy(out=b1[:], in_=b1_raw[:])
         transpose_x(0)
         quantise_x(0)
-        transpose_x(1)
-        quantise_x(1)
         sort_w1_scales(1)
         sort_w1(0, 1, 1)
+        transpose_x(1)
+        quantise_x(1)
         for k in range(-1, STEPS + 1):
             x_step, l1_step, y_step, o_step = k + 2, k + 1, k, k - 1
             has_x = 1 < x_step < STEPS
@@ -267,13 +290,18 @@ def tile_dummytemodel_pa_t_e_kernel(
                 if j == 0 and has_x:
                     transpose_x(x_step)
                 if has_l1:
-                    for i in (2 * j, 2 * j + 1):
-                        layer1(l1_step, i // PACK, i % PACK)
+                    if l1_step < DIRECT_STEPS:
+                        if j < MID_PASSES:
+                            for i in range(STEP_LIST[l1_step][2]):
+                                layer1_direct(l1_step, j, i)
+                    else:
+                        for i in (2 * j, 2 * j + 1):
+                            layer1(l1_step, i // PACK, i % PACK)
                 if j < o_tiles:
                     layer2(o_step, j)
                 if j == 0 and l1_step + 1 < STEPS and STEP_LIST[l1_step + 1][1] == 0:
                     sort_w1(STEP_LIST[l1_step + 1][0], 0, MID_PASSES)
-                if j < 2 and has_y:
+                if j < 2 and has_y and DIRECT_STEPS <= y_step:
                     group_y(y_step, j)
                 if j == 2 and has_y:
                     quantise_y(y_step, 0)

@@ -9,6 +9,7 @@ I32 = mybir.dt.int32
 U32 = mybir.dt.uint32
 U8 = mybir.dt.uint8
 FP8X4 = mybir.dt.float8_e4m3fn_x4
+MULT = mybir.AluOpType.mult
 ADD = mybir.AluOpType.add
 IDENTITY = mybir.ActivationFunctionType.Identity
 
@@ -204,7 +205,7 @@ def tile_dummytemodel_pa_t_e_kernel(
         def layer1_direct(s, c, j):
             e, first, tiles = STEP_LIST[s]
             if j == 0:
-                y_grouped[s, c] = work.tile([P, tiles * P, PACK], BF16, align_bytes=64, name="y_grouped", bufs=4)
+                y_grouped[s, c] = work.tile([P, tiles * P, PACK], BF16, align_bytes=64, name="y_grouped", bufs=2)
             y_ps = psum_y.tile([P, PACK, P], F32, tag="y")
             for t in range(PACK):
                 nc.tensor.matmul_mx(
@@ -223,17 +224,26 @@ def tile_dummytemodel_pa_t_e_kernel(
                 op=ADD,
             )
 
-        def group_y(s, c):
-            tokens = STEP_LIST[s][2] * P
-            y_grouped[s, c] = work.tile([P, tokens, PACK], BF16, align_bytes=64, name="y_grouped", bufs=4)
+        def group_parts(s, c):
+            blocks = STEP_LIST[s][2] * P // RUN
+            share = 16 if s >= 8 else 8 if s >= 5 else 0
+            d = blocks - blocks * share // 32
+            b = d - blocks * 4 // 32
             dst = y_grouped[s, c][:].rearrange("p (k i) t -> p k t i", i=RUN)
             src = y_plain[s, c][:].rearrange("p t (k i) -> p k t i", i=RUN)
-            blocks = tokens // RUN
-            share = 16 if s >= 8 else 8 if s >= 5 else 0
-            scalar_from = blocks - blocks * share // 32
-            nc.vector.tensor_copy(out=dst[:, :scalar_from], in_=src[:, :scalar_from])
-            if scalar_from < blocks:
-                nc.scalar.copy(out=dst[:, scalar_from:], in_=src[:, scalar_from:])
+            return blocks, b, d, dst, src
+
+        def group_y_ahead(s, c):
+            tokens = STEP_LIST[s][2] * P
+            y_grouped[s, c] = work.tile([P, tokens, PACK], BF16, align_bytes=64, name="y_grouped", bufs=2)
+            blocks, b, d, dst, src = group_parts(s, c)
+            nc.gpsimd.tensor_scalar(out=dst[:, b:d], in0=src[:, b:d], scalar1=1.0, scalar2=0.0, op0=MULT, op1=ADD)
+
+        def group_y(s, c):
+            blocks, b, d, dst, src = group_parts(s, c)
+            nc.vector.tensor_copy(out=dst[:, :b], in_=src[:, :b])
+            if d < blocks:
+                nc.scalar.copy(out=dst[:, d:], in_=src[:, d:])
 
         def quantise_y(s, c):
             tokens = STEP_LIST[s][2] * P
@@ -272,10 +282,10 @@ def tile_dummytemodel_pa_t_e_kernel(
                 nc.sync.dma_start(out=out_tiles[e][:, first + j - pair + 1 : first + j + 1, :], in_=o_sb[s][:])
 
         sort_w1_scales(0)
-        sort_w1(0, 0, 1)
         nc.gpsimd.tensor_copy(out=b1[:], in_=b1_raw[:])
         transpose_x(0)
         quantise_x(0)
+        sort_w1(0, 0, 1)
         sort_w1_scales(1)
         sort_w1(0, 1, 1)
         transpose_x(1)
@@ -305,10 +315,14 @@ def tile_dummytemodel_pa_t_e_kernel(
                     group_y(y_step, j)
                 if j == 2 and has_y:
                     quantise_y(y_step, 0)
+                    if y_step + 1 < STEPS:
+                        group_y_ahead(y_step + 1, 0)
                 if j == 2 and has_x:
                     quantise_x(x_step)
                 if j == 3 and has_y:
                     quantise_y(y_step, 1)
+                    if y_step + 1 < STEPS:
+                        group_y_ahead(y_step + 1, 1)
                 if j < o_tiles and y_step != STEPS - 1:
                     finish(o_step, j)
             if y_step == STEPS - 1:

@@ -282,10 +282,10 @@ def tile_dummytemodel_pa_t_e_kernel(
                 nc.sync.dma_start(out=out_tiles[e][:, first + j - pair + 1 : first + j + 1, :], in_=o_sb[s][:])
 
         sort_w1_scales(0)
+        sort_w1(0, 0, 1)
         nc.gpsimd.tensor_copy(out=b1[:], in_=b1_raw[:])
         transpose_x(0)
         quantise_x(0)
-        sort_w1(0, 0, 1)
         sort_w1_scales(1)
         sort_w1(0, 1, 1)
         transpose_x(1)

from contextlib import ExitStack

import concourse.mybir as mybir
from concourse.masks import make_identity

F32 = mybir.dt.float32
BF16 = mybir.dt.bfloat16
I32 = mybir.dt.int32
U32 = mybir.dt.uint32
U8 = mybir.dt.uint8
FP8X4 = mybir.dt.float8_e4m3fn_x4
MULT = mybir.AluOpType.mult
ADD = mybir.AluOpType.add
IDENTITY = mybir.ActivationFunctionType.Identity

P = 128
PACK = 4
K_PASS = P * PACK
GROUPS = 4
HID = 512
MID = 1024
MID_PASSES = MID // K_PASS
TILES = 1024 // P
STEP_TILES = ((2, 2, 4), (4, 4), (4, 4), (4, 2, 2))
STEP_LIST = [(e, sum(widths[:i]), w) for e, widths in enumerate(STEP_TILES) for i, w in enumerate(widths)]
STEPS = len(STEP_LIST)

WARM_UP = 3
DIRECT_STEPS = 1
RUN = 4

FLOPS = 2 * GROUPS * 1024 * (HID * MID + MID * HID)


def tile_dummytemodel_pa_t_e_kernel(
    tc, hf, g1_w_words, g1_w_scales, g1_b, g2_w_words, g2_w_scales, g2_b, out
):
    nc = tc.nc
    hf_tiles = hf.rearrange("(e p i) k -> e p i k", e=GROUPS, i=TILES)
    out_tiles = out.rearrange("(e p i) n -> e p i n", e=GROUPS, i=TILES)

    with ExitStack() as ctx:
        keep = ctx.enter_context(tc.tile_pool(name="keep", bufs=1))
        work = ctx.enter_context(tc.tile_pool(name="work", bufs=2))
        psum_x = ctx.enter_context(tc.psum_pool(name="psum_x", bufs=2))
        psum_y = ctx.enter_context(tc.psum_pool(name="psum_y", bufs=4))
        psum_o = ctx.enter_context(tc.psum_pool(name="psum_o", bufs=2))
        ctx.enter_context(tc.manual_schedule())

        x_sb = keep.tile([P, GROUPS, TILES, HID], BF16)
        w1_raw = keep.tile([P, GROUPS, MID], U32, align_bytes=64)
        w1 = keep.tile([P, GROUPS, MID_PASSES, PACK, P], U32, align_bytes=64)
        w2 = keep.tile([P, GROUPS, MID_PASSES, HID], U32, align_bytes=64)
        w1_scales_raw = keep.tile([P, MID], U8, align_bytes=64)
        w1_scales = keep.tile([P, MID_PASSES, PACK, P], U8, align_bytes=64)
        w2_scales = keep.tile([P, GROUPS // 2, HID], U8, align_bytes=64)
        b1_raw = keep.tile([P, GROUPS * MID_PASSES, PACK], BF16)
        b1 = keep.tile([P, GROUPS * MID_PASSES, PACK], F32)
        b2_rows = keep.tile([P, GROUPS, HID], BF16)
        ident_f32 = keep.tile([P, P], F32)

        zeros = keep.tile([P, HID], BF16)
        nc.vector.memset(zeros[:], 0.0)
        nc.vector.memset(w1_scales_raw[:].bitcast(I32), 0)
        nc.vector.memset(w2_scales[:].bitcast(I32), 0)
        make_identity(nc, ident_f32[:])

        idle_ps = psum_o.tile([P, HID], F32, tag="o", name="o_ps")
        for i in range(WARM_UP):
            nc.tensor.matmul(out=idle_ps[:], lhsT=zeros[:, :P], rhs=zeros[:], start=True, stop=True)

        def load_tokens(e, first, count):
            nc.sync.dma_start(out=x_sb[:, e, first : first + count, :], in_=hf_tiles[e][:, first : first + count, :])

        def load_w1(e, first, count):
            columns = slice(K_PASS * first, K_PASS * (first + count))
            nc.sync.dma_start(
                out=w1_raw[:, e, columns].bitcast(I32),
                in_=g1_w_words[e][:, columns, :].rearrange("p n t -> p (n t)").bitcast(I32),
            )

        def load_w2(e):
            nc.sync.dma_start(
                out=w2[:, e, :, :].bitcast(I32),
                in_=g2_w_words[MID_PASSES * e : MID_PASSES * (e + 1)].rearrange("c p n t -> p c (n t)").bitcast(I32),
            )

        def load_w1_scales():
            for quadrant in range(4):
                rows = slice(4 * quadrant, 4 * quadrant + 4)
                nc.sync.dma_start(
                    out=w1_scales_raw[32 * quadrant : 32 * quadrant + 16, :].bitcast(I32),
                    in_=g1_w_scales[:, rows, :].bitcast(I32),
                )

        def load_w2_scales(h):
            for quadrant in range(4):
                rows = slice(4 * quadrant, 4 * quadrant + 4)
                nc.sync.dma_start(
                    out=w2_scales[32 * quadrant : 32 * quadrant + 16, h, :].bitcast(I32),
                    in_=g2_w_scales[4 * h : 4 * h + 4, rows, :].bitcast(I32),
                )

        def load_b1():
            nc.sync.dma_start(out=b1_raw[:], in_=g1_b.rearrange("e (c p t) -> p (e c) t", c=MID_PASSES, t=PACK))

        def load_b2(e):
            nc.sync.dma_start(out=b2_rows[:, e, :], in_=g2_b[e].partition_broadcast(P))

        def load_b2_all():
            nc.sync.dma_start(
                out=b2_rows[:].rearrange("q e n -> q (e n)"), in_=g2_b.rearrange("e n -> (e n)").partition_broadcast(P)
            )

        load_tokens(0, 0, 2)
        load_tokens(0, 2, 2)
        load_w1_scales()
        load_w1(0, 0, 1)
        load_b1()
        load_w1(0, 1, 1)
        load_tokens(0, 4, 4)
        load_w2(0)
        load_tokens(1, 0, 4)
        load_w2_scales(0)
        load_w1(1, 0, MID_PASSES)
        load_b2_all()
        load_tokens(1, 4, 4)
        load_w2(1)
        load_w1(2, 0, MID_PASSES)
        load_tokens(2, 0, TILES)
        load_w2_scales(1)
        load_w2(2)
        load_w1(3, 0, MID_PASSES)
        load_tokens(3, 0, TILES)
        load_w2(3)

        x_grouped = {}
        x_codes = {}
        x_scales = {}
        y_plain = {}
        y_grouped = {}
        y_codes = {}
        y_scales = {}
        o_sb = {}
        o_ps = {}

        def sort_w1_scales(c):
            nc.vector.tensor_copy(
                out=w1_scales[:, c],
                in_=w1_scales_raw[:, K_PASS * c : K_PASS * (c + 1)].rearrange("p (m t) -> p t m", t=PACK),
            )

        def sort_w1(e, first, count):
            nc.vector.tensor_copy(
                out=w1[:, e, first : first + count].bitcast(I32),
                in_=w1_raw[:, e, K_PASS * first : K_PASS * (first + count)]
                .bitcast(I32)
                .rearrange("p (c m t) -> p c t m", c=count, t=PACK),
            )

        def transpose_x(s):
            e, first, tiles = STEP_LIST[s]
            x_grouped[s] = work.tile([P, tiles * P * PACK], BF16, align_bytes=64, name="x_grouped", bufs=2)
            for h in range(0, tiles, 2):
                pair = min(2, tiles - h)
                x_t = psum_x.tile([P, pair, 2, P], F32, tag="x")
                for j in range(pair):
                    words = x_sb[:, e, first + h + j, :].bitcast(F32)
                    for u in range(2):
                        nc.tensor.transpose(out=x_t[:, j, u, :], in_=words[:, u : HID // 2 : 2], identity=ident_f32[:])
                copy_x = nc.scalar.copy
                copy_x(
                    out=x_grouped[s][:, K_PASS * h : K_PASS * (h + pair)]
                    .bitcast(F32)
                    .rearrange("p (j r u) -> p j r u", j=pair, u=2),
                    in_=x_t[:].rearrange("p j u r -> p j r u"),
                )

        def quantise_x(s):
            tokens = STEP_LIST[s][2] * P
            x_codes[s] = work.tile([P, tokens], U32, align_bytes=64, name="x_codes", bufs=3)
            x_scales[s] = work.tile([P, tokens], U8, align_bytes=64, name="x_scales", bufs=3)
            nc.vector.quantize_mx(out=x_codes[s][:].bitcast(FP8X4), scales=x_scales[s][:], in_=x_grouped[s][:])

        def layer1(s, c, t):
            e, first, tiles = STEP_LIST[s]
            tokens = tiles * P
            if t == 0:
                y_plain[s, c] = work.tile([P, PACK, tokens], BF16, align_bytes=64, name="y_plain", bufs=4)
            y_ps = psum_y.tile([P, tokens], F32, tag="y")
            nc.tensor.matmul_mx(
                out=y_ps[:],
                lhsT=w1[:, e, c, t, :].bitcast(FP8X4),
                lhsT_scale=w1_scales[4 * e : P, c, t, :],
                rhs=x_codes[s][:].bitcast(FP8X4),
                rhs_scale=x_scales[s][:],
                start=True,
                stop=True,
            )
            column = MID_PASSES * e + c
            nc.scalar.activation(
                out=y_plain[s, c][:, t, :], in_=y_ps[:], func=IDENTITY, bias=b1[:, column, t : t + 1], scale=1.0
            )

        def layer1_direct(s, c, j):
            e, first, tiles = STEP_LIST[s]
            if j == 0:
                y_grouped[s, c] = work.tile([P, tiles * P, PACK], BF16, align_bytes=64, name="y_grouped", bufs=2)
            y_ps = psum_y.tile([P, PACK, P], F32, tag="y")
            for t in range(PACK):
                nc.tensor.matmul_mx(
                    out=y_ps[:, t, :],
                    lhsT=w1[:, e, c, t, :].bitcast(FP8X4),
                    lhsT_scale=w1_scales[4 * e : P, c, t, :],
                    rhs=x_codes[s][:, P * j : P * (j + 1)].bitcast(FP8X4),
                    rhs_scale=x_scales[s][:, P * j : P * (j + 1)],
                    start=True,
                    stop=True,
                )
            nc.vector.tensor_tensor(
                out=y_grouped[s, c][:, P * j : P * (j + 1), :],
                in0=y_ps[:].rearrange("p t n -> p n t"),
                in1=b1[:, MID_PASSES * e + c, :].unsqueeze(1).to_broadcast([P, P, PACK]),
                op=ADD,
            )

        def group_parts(s, c):
            blocks = STEP_LIST[s][2] * P // RUN
            share = 16 if s >= 8 else 8 if s >= 5 else 0
            d = blocks - blocks * share // 32
            b = d - blocks * 4 // 32
            dst = y_grouped[s, c][:].rearrange("p (k i) t -> p k t i", i=RUN)
            src = y_plain[s, c][:].rearrange("p t (k i) -> p k t i", i=RUN)
            return blocks, b, d, dst, src

        def group_y_ahead(s, c):
            tokens = STEP_LIST[s][2] * P
            y_grouped[s, c] = work.tile([P, tokens, PACK], BF16, align_bytes=64, name="y_grouped", bufs=2)
            blocks, b, d, dst, src = group_parts(s, c)
            nc.gpsimd.tensor_scalar(out=dst[:, b:d], in0=src[:, b:d], scalar1=1.0, scalar2=0.0, op0=MULT, op1=ADD)

        def group_y(s, c):
            blocks, b, d, dst, src = group_parts(s, c)
            nc.vector.tensor_copy(out=dst[:, :b], in_=src[:, :b])
            if d < blocks:
                nc.scalar.copy(out=dst[:, d:], in_=src[:, d:])

        def quantise_y(s, c):
            tokens = STEP_LIST[s][2] * P
            y_codes[s, c] = work.tile([P, tokens], U32, align_bytes=64, name="y_codes", bufs=4)
            y_scales[s, c] = work.tile([P, tokens], U8, align_bytes=64, name="y_scales", bufs=4)
            nc.vector.quantize_mx(
                out=y_codes[s, c][:].bitcast(FP8X4),
                scales=y_scales[s, c][:],
                in_=y_grouped[s, c][:].rearrange("p n t -> p (n t)"),
            )

        def layer2(s, j):
            e = STEP_LIST[s][0]
            if s == STEPS - 1:
                o_ps[s, j] = psum_y.tile([P, HID], F32, tag="y", name="y_ps")
            else:
                o_ps[s, j] = psum_o.tile([P, HID], F32, tag="o", name="o_ps")
            for c in range(MID_PASSES):
                nc.tensor.matmul_mx(
                    out=o_ps[s, j][:],
                    lhsT=y_codes[s, c][:, P * j : P * (j + 1)].bitcast(FP8X4),
                    lhsT_scale=y_scales[s, c][:, P * j : P * (j + 1)],
                    rhs=w2[:, e, c, :].bitcast(FP8X4),
                    rhs_scale=w2_scales[4 * (MID_PASSES * (e % 2) + c) : P, e // 2, :],
                    start=(c == 0),
                    stop=(c == MID_PASSES - 1),
                )

        def finish(s, j):
            e, first, tiles = STEP_LIST[s]
            pair = 1 if s == STEPS - 1 else min(2, tiles)
            if j % pair == 0:
                o_sb[s] = work.tile([P, pair, HID], F32, name="o_sb", bufs=6)
            nc.vector.tensor_tensor(out=o_sb[s][:, j % pair, :], in0=o_ps[s, j][:], in1=b2_rows[:, e, :], op=ADD)
            if j % pair == pair - 1:
                nc.sync.dma_start(out=out_tiles[e][:, first + j - pair + 1 : first + j + 1, :], in_=o_sb[s][:])

        sort_w1_scales(0)
        sort_w1(0, 0, 1)
        nc.gpsimd.tensor_copy(out=b1[:], in_=b1_raw[:])
        transpose_x(0)
        quantise_x(0)
        sort_w1_scales(1)
        sort_w1(0, 1, 1)
        transpose_x(1)
        quantise_x(1)
        for k in range(-1, STEPS + 1):
            x_step, l1_step, y_step, o_step = k + 2, k + 1, k, k - 1
            has_x = 1 < x_step < STEPS
            has_l1 = l1_step < STEPS
            has_y = 0 <= y_step < STEPS
            o_tiles = STEP_LIST[o_step][2] if 0 <= o_step else 0
            for j in range(4):
                if j == 0 and has_x:
                    transpose_x(x_step)
                if has_l1:
                    if l1_step < DIRECT_STEPS:
                        if j < MID_PASSES:
                            for i in range(STEP_LIST[l1_step][2]):
                                layer1_direct(l1_step, j, i)
                    else:
                        for i in (2 * j, 2 * j + 1):
                            layer1(l1_step, i // PACK, i % PACK)
                if j < o_tiles:
                    layer2(o_step, j)
                if j == 0 and l1_step + 1 < STEPS and STEP_LIST[l1_step + 1][1] == 0:
                    sort_w1(STEP_LIST[l1_step + 1][0], 0, MID_PASSES)
                if j < 2 and has_y and DIRECT_STEPS <= y_step:
                    group_y(y_step, j)
                if j == 2 and has_y:
                    quantise_y(y_step, 0)
                    if y_step + 1 < STEPS:
                        group_y_ahead(y_step + 1, 0)
                if j == 2 and has_x:
                    quantise_x(x_step)
                if j == 3 and has_y:
                    quantise_y(y_step, 1)
                    if y_step + 1 < STEPS:
                        group_y_ahead(y_step + 1, 1)
                if j < o_tiles and y_step != STEPS - 1:
                    finish(o_step, j)
            if y_step == STEPS - 1:
                for j in range(o_tiles):
                    finish(o_step, j)
